import numpy as np
import ml_dtypes


def mxq(x, axis, fmt="e4m3"):
    dtype, down = {"e4m3": (ml_dtypes.float8_e4m3fn, 7), "e5m2": (ml_dtypes.float8_e5m2, 14)}[fmt]
    v = np.moveaxis(np.asarray(x, np.float32).astype(ml_dtypes.bfloat16).astype(np.float64), axis, -1)
    blocks = v.reshape(v.shape[:-1] + (-1, 32))
    amax = np.abs(blocks).max(-1, keepdims=True)
    byte = np.maximum(np.where(amax > 0, np.frexp(amax)[1] - 1 + 127, 0) - down, 1)
    scale = np.exp2(byte - 127.0)
    codes = (blocks / scale).astype(np.float32).astype(dtype).astype(np.float64)
    return np.moveaxis((codes * scale).reshape(v.shape), -1, axis)


WIDE = False


def mx_kscale(k):
    if not WIDE:
        return np.ones(k)
    levels = np.array([10, -10, 5, -5, 0])
    a = np.random.permutation(np.resize(levels, k // 512 * 4)).reshape(k // 512, 4)
    idx = np.arange(k)
    return np.exp2(a[idx // 512, idx % 128 // 32])


BF16 = ml_dtypes.bfloat16


def bf(x):
    return np.asarray(x, np.float32).astype(BF16)


def f64(x):
    return np.asarray(x).astype(np.float64)


E2M1 = np.array([0.0, 0.5, 1.0, 1.5, 2.0, 3.0, 4.0, 6.0, -0.0, -0.5, -1.0, -1.5, -2.0, -3.0, -4.0, -6.0])


def pack_weight(w, fmt):
    k, n = w.shape
    w = f64(bf(w)).reshape(k // 32, 32, n)
    amax = np.abs(w).max(1)
    if fmt == "e4m3":
        byte = np.frexp(amax)[1] - 1 + 127 - 7
    else:
        mant, ex = np.frexp(amax / 6.0)
        byte = np.where(mant > 0.5, ex, ex - 1) + 127
    byte = np.clip(np.where(amax > 0, byte, 1), 1, 254)
    scaled = (w * np.exp2(127.0 - byte)[:, None, :]).reshape(k, n).astype(np.float32)
    by_word = np.ascontiguousarray(scaled.reshape(k // 512, 128, 4, n).transpose(0, 1, 3, 2))
    if fmt == "e4m3":
        words = by_word.astype(ml_dtypes.float8_e4m3fn).view(np.uint8)
    else:
        c = by_word.astype(ml_dtypes.float4_e2m1fn).view(np.uint8) & 0xF
        words = c[..., 0::2] | (c[..., 1::2] << 4)
    return np.ascontiguousarray(words), np.ascontiguousarray(byte.astype(np.uint8).reshape(k // 512, 16, n))


def unpack_weight(words, scales, fmt):
    g, p, n, _ = words.shape
    if fmt == "e4m3":
        vals = np.ascontiguousarray(words).view(ml_dtypes.float8_e4m3fn).astype(np.float64)
    else:
        nib = np.empty((g, p, n, 4), np.uint8)
        nib[..., 0::2] = words & 0xF
        nib[..., 1::2] = words >> 4
        vals = E2M1[nib]
    vals = vals * np.repeat(np.exp2(scales.astype(np.float64) - 127.0), 8, axis=1)[..., None]
    return vals.transpose(0, 1, 3, 2).reshape(g * 512, n)


B, Nx, Nh, Ny, G = 128, 16384, 1024, 2048, 4
NU = 1.0


def setup_inputs():
    s = mx_kscale(Nx)
    base = np.random.standard_normal((G, Nx))
    w = np.random.standard_normal((Nh, Nx)) * np.sqrt(24.0 / (Nx * Nh))
    b = np.random.standard_normal(Nh) * 2.0 / np.sqrt(Nh)
    hid = np.stack([np.maximum((w * np.maximum(base[g], 0.0)).sum(axis=1) + b, 0.0) for g in range(G)])
    x = np.sqrt(0.75) * base[np.random.randint(0, G, B)] + 0.5 * np.random.standard_normal((B, Nx))
    wq = np.random.uniform(0.5, 1.5, (Ny, 1)) * hid[np.random.randint(0, G, Ny)] + np.random.standard_normal((Ny, Nh)) / np.sqrt(Nh)
    words, scales = pack_weight((w / s[None, :]).T, "e4m3")
    return {"x": bf(x * s),
            "W_fc_words": words,
            "W_fc_scales": scales,
            "b_fc": bf(b),
            "W_q": bf(wq)}


def reference(x, W_fc_words, W_fc_scales, b_fc, W_q):
    wq = f64(W_q)
    a = np.maximum(f64(x), 0.0)
    h = np.maximum((mxq(a, 1, "e4m3") @ unpack_weight(W_fc_words, W_fc_scales, "e4m3")) + f64(b_fc), 0.0)
    d = (np.sum(h * h, axis=-1, keepdims=True)
         - 2.0 * (mxq(h, 1, "e4m3") @ mxq(wq, 1, "e4m3").T)
         + np.sum(wq * wq, axis=-1))
    d = np.maximum(d, 0.0)
    t = (-(NU + 1.0) / 2.0) * np.log1p(d / NU)
    m = t.max(axis=-1, keepdims=True)
    return t - (m + np.log(np.sum(np.exp(t - m), axis=-1, keepdims=True)))

@@ -1,0 +1,301 @@
+from contextlib import ExitStack
+
+import concourse.mybir as mybir
+from concourse.masks import make_identity
+
+BF16 = mybir.dt.bfloat16
+F32 = mybir.dt.float32
+I32 = mybir.dt.int32
+U32 = mybir.dt.uint32
+U8 = mybir.dt.uint8
+FP8X4 = mybir.dt.float8_e4m3fn_x4
+ALU = mybir.AluOpType
+ACT = mybir.ActivationFunctionType
+AXIS = mybir.AxisListType
+
+P = 128
+PACK = 4
+K_PASS = P * PACK
+WORDS = K_PASS // 2
+BANK = 512
+
+NX = 16384
+NH = 1024
+NY = 2048
+X_PASSES = NX // K_PASS
+H_PASSES = NH // K_PASS
+Y_BANKS = NY // BANK
+
+SLOT = 4096
+X_CHUNKS = NX // SLOT
+TILE_UNITS = 4
+ROWS_PER_PARTITION = 4
+W_CHUNK_PASSES = 2
+W_CHUNKS = X_PASSES // W_CHUNK_PASSES
+W_BUFFERS = 8
+PLANES_PER_TILE = 4
+NORMS_AFTER_CHUNK = 3 * W_CHUNKS // 4
+
+FLOPS = 2 * P * NX * NH + 2 * P * NH * NY
+
+
+def tile_tnet_k_kernel(tc, x, W_fc_words, W_fc_scales, b_fc, W_q, out):
+    nc = tc.nc
+    with ExitStack() as ctx:
+        ctx.enter_context(tc.manual_schedule())
+        keep = ctx.enter_context(tc.tile_pool(name="keep", bufs=1))
+        large = ctx.enter_context(tc.tile_pool(name="large", bufs=8))
+        stream = ctx.enter_context(tc.tile_pool(name="stream", bufs=W_BUFFERS))
+        stage = ctx.enter_context(tc.tile_pool(name="stage", bufs=3))
+        h_banks = ctx.enter_context(tc.psum_pool(name="h_banks", bufs=1))
+        banks = ctx.enter_context(tc.psum_pool(name="banks", bufs=6))
+
+        w_planes = keep.tile([P, X_PASSES // PLANES_PER_TILE, NH], U8, align_bytes=64)
+        nc.vector.memset(w_planes[:].bitcast(I32), 0)
+        ones = keep.tile([P, P], BF16)
+        nc.vector.memset(ones[:], 1.0)
+        bias_rows = keep.tile([P, NH], BF16)
+        nc.vector.memset(bias_rows[:], 0.0)
+        nc.scalar.dma_start(out=bias_rows[0:1, :], in_=b_fc.rearrange("(o n) -> o n", o=1))
+        ident_f32 = keep.tile([P, P], F32)
+        make_identity(nc, ident_f32[:])
+        ident_bf16 = keep.tile([P, P], BF16)
+        make_identity(nc, ident_bf16[:])
+        warm = keep.tile([P, 1], F32)
+        nc.scalar.activation(out=warm[:], in_=ones[:, 0:1], func=ACT.Ln)
+
+        x_chunks = []
+        for c in range(X_CHUNKS):
+            x_chunk = large.tile([P, SLOT], BF16, tag="large", name="x_chunk%d" % c)
+            nc.sync.dma_start(out=x_chunk[:], in_=x[:, SLOT * c : SLOT * (c + 1)])
+            x_chunks.append(x_chunk)
+
+        scale_rows = W_fc_scales.bitcast(I32).rearrange("(a i) q n -> q i a n", i=PLANES_PER_TILE)
+        planes_i32 = w_planes[:].bitcast(I32)
+        for quadrant in range(4):
+            for r in range(4):
+                first = 32 * quadrant + r
+                nc.sync.dma_start(
+                    out=planes_i32[first : first + 4 * PLANES_PER_TILE : 4],
+                    in_=scale_rows[4 * quadrant + r],
+                )
+
+        wq_chunks = []
+        for T in range(Y_BANKS):
+            wq_chunk = large.tile([P, ROWS_PER_PARTITION, NH], BF16, tag="large", name="wq_chunk%d" % T)
+            nc.sync.dma_start(
+                out=wq_chunk[:],
+                in_=W_q[BANK * T : BANK * (T + 1), :].rearrange("(p s) k -> p s k", s=ROWS_PER_PARTITION),
+            )
+            wq_chunks.append(wq_chunk)
+
+        w_words_dram = W_fc_words.rearrange("g p n t -> p g (n t)").bitcast(I32)
+        w_chunks = []
+
+        def load_w_chunk(c):
+            w_chunk = stream.tile([P, W_CHUNK_PASSES, NH], U32, tag="w_chunk", name="w_chunk%d" % c, align_bytes=64)
+            nc.sync.dma_start(
+                out=w_chunk[:].bitcast(I32),
+                in_=w_words_dram[:, W_CHUNK_PASSES * c : W_CHUNK_PASSES * (c + 1), :],
+            )
+            w_chunks.append(w_chunk)
+
+        for c in range(W_BUFFERS):
+            load_w_chunk(c)
+
+        def regroup(units):
+            grouped = stage.tile([P, TILE_UNITS * K_PASS], BF16, tag="grouped", align_bytes=64)
+            grouped_words = grouped[:].bitcast(F32).rearrange("p (c r u) -> p c r u", c=TILE_UNITS, u=2)
+            for pair in range(TILE_UNITS // 2):
+                bank = banks.tile([P, 2, 2, P], F32, tag="bank")
+                for i in range(2):
+                    for u in range(2):
+                        nc.tensor.transpose(bank[:, i, u, :], units[2 * pair + i][:, u:WORDS:2], ident_f32[:])
+                source = bank[:].rearrange("p c u r -> p c r u")
+                target = grouped_words[:, 2 * pair : 2 * pair + 2]
+                if pair == 0:
+                    nc.vector.tensor_copy(out=target, in_=source)
+                else:
+                    nc.scalar.copy(out=target, in_=source)
+            return grouped
+
+        def quantise(grouped, codes, scales):
+            nc.vector.quantize_mx(out=codes.bitcast(FP8X4), scales=scales, in_=grouped[:])
+
+        a_codes = keep.tile([P, X_PASSES, P], U32, align_bytes=64)
+        a_scales = keep.tile([P, X_PASSES, P], U8, align_bytes=64)
+        wq_codes = keep.tile([P, H_PASSES, NY], U32, align_bytes=64)
+        wq_scales = keep.tile([P, H_PASSES, NY], U8, align_bytes=64)
+
+        waiting = None
+        for c in range(X_CHUNKS):
+            x_chunk = x_chunks[c]
+            nc.vector.tensor_scalar_max(out=x_chunk[:], in0=x_chunk[:], scalar1=0.0)
+            x_words = x_chunk[:].bitcast(F32)
+            for first in range(0, SLOT // K_PASS, TILE_UNITS):
+                grouped = regroup([x_words[:, WORDS * (first + i) : WORDS * (first + i + 1)] for i in range(TILE_UNITS)])
+                if waiting is not None:
+                    quantise(*waiting)
+                g = (SLOT // K_PASS) * c + first
+                waiting = (
+                    grouped,
+                    a_codes[:, g : g + TILE_UNITS, :].rearrange("p g b -> p (g b)"),
+                    a_scales[:, g : g + TILE_UNITS, :].rearrange("p g b -> p (g b)"),
+                )
+        for T in range(Y_BANKS):
+            wq_words = wq_chunks[T][:].bitcast(F32)
+            for g in range(H_PASSES):
+                grouped = regroup([wq_words[:, s, WORDS * g : WORDS * (g + 1)] for s in range(ROWS_PER_PARTITION)])
+                quantise(*waiting)
+                waiting = (
+                    grouped,
+                    wq_codes[:, g, BANK * T : BANK * (T + 1)],
+                    wq_scales[:, g, BANK * T : BANK * (T + 1)],
+                )
+        quantise(*waiting)
+
+        bias_sorted = keep.tile([P, H_PASSES, PACK, P], F32)
+        for g in range(H_PASSES):
+            bias_bank = banks.tile([P, BANK], F32, tag="bank", name="bias_bank%d" % g)
+            nc.tensor.matmul(
+                out=bias_bank[:], lhsT=ones[:], rhs=bias_rows[:, BANK * g : BANK * (g + 1)], start=True, stop=True
+            )
+            nc.scalar.copy(out=bias_sorted[:, g], in_=bias_bank[:].rearrange("b (p t) -> b t p", t=PACK))
+
+        wq_norms = keep.tile([P, Y_BANKS * ROWS_PER_PARTITION], F32)
+        for T in range(Y_BANKS):
+            for s in range(ROWS_PER_PARTITION):
+                squares = stage.tile([P, NH], BF16, tag="squares")
+                column = ROWS_PER_PARTITION * T + s
+                nc.scalar.activation(
+                    out=squares[:], in_=wq_chunks[T][:, s, :], func=ACT.Square, accum_out=wq_norms[:, column : column + 1]
+                )
+
+        h_acc = [h_banks.tile([P, BANK], F32, name="h_acc%d" % n) for n in range(H_PASSES)]
+        norms_plus_1 = None
+        for c in range(W_CHUNKS):
+            for i in range(W_CHUNK_PASSES):
+                g = W_CHUNK_PASSES * c + i
+                plane_start = 4 * (g % PLANES_PER_TILE)
+                for n in range(H_PASSES):
+                    columns = slice(BANK * n, BANK * (n + 1))
+                    nc.tensor.matmul_mx(
+                        out=h_acc[n][:],
+                        lhsT=a_codes[:, g, :].bitcast(FP8X4),
+                        lhsT_scale=a_scales[:, g, :],
+                        rhs=w_chunks[c][:, i, columns].bitcast(FP8X4),
+                        rhs_scale=w_planes[plane_start:P, g // PLANES_PER_TILE, columns],
+                        start=(g == 0),
+                        stop=(g == X_PASSES - 1),
+                    )
+            if c + W_BUFFERS < W_CHUNKS:
+                load_w_chunk(c + W_BUFFERS)
+
+            if c == NORMS_AFTER_CHUNK:
+                norms_plus_1 = large.tile([P, Y_BANKS, BANK], F32, tag="large")
+                for T in range(Y_BANKS):
+                    norm_bank = banks.tile([P, ROWS_PER_PARTITION, P], F32, tag="bank")
+                    for s in range(ROWS_PER_PARTITION):
+                        column = ROWS_PER_PARTITION * T + s
+                        nc.tensor.transpose(
+                            norm_bank[:, s, :], wq_norms[:, column : column + 1].to_broadcast([P, P]), ident_f32[:]
+                        )
+                    nc.vector.tensor_scalar_add(
+                        out=norms_plus_1[:, T, :].rearrange("b (p s) -> b p s", s=ROWS_PER_PARTITION),
+                        in0=norm_bank[:].rearrange("b s p -> b p s"),
+                        scalar1=1.0,
+                    )
+
+        pre = keep.tile([P, H_PASSES, PACK, P], F32)
+        h_bf16 = keep.tile([P, H_PASSES, PACK, P], BF16)
+        h_squares = keep.tile([P, H_PASSES, K_PASS], F32)
+        h_norm_parts = keep.tile([P, H_PASSES], F32)
+        h_grouped = keep.tile([P, H_PASSES, P, PACK], BF16, align_bytes=64)
+        h_codes = keep.tile([P, H_PASSES, P], U32, align_bytes=64)
+        h_scales = keep.tile([P, H_PASSES, P], U8, align_bytes=64)
+
+        def sum_h_squares(g):
+            flat = pre[:, g].rearrange("b t p -> b (t p)")
+            nc.vector.scalar_tensor_tensor(
+                out=h_squares[:, g, :], in0=flat, scalar=0.0, in1=flat, op0=ALU.max, op1=ALU.mult,
+                accum_out=h_norm_parts[:, g : g + 1],
+            )
+
+        for g in range(H_PASSES):
+            nc.vector.tensor_tensor(
+                out=pre[:, g], in0=h_acc[g][:].rearrange("b (p t) -> b t p", t=PACK), in1=bias_sorted[:, g], op=ALU.add
+            )
+            nc.scalar.activation(out=h_bf16[:, g], in_=pre[:, g], func=ACT.Relu)
+        sum_h_squares(0)
+        h_T = []
+        for g in range(H_PASSES):
+            h_T_bank = banks.tile([P, PACK, P], BF16, tag="bank", name="h_T_bank%d" % g)
+            for t in range(PACK):
+                nc.tensor.transpose(h_T_bank[:, t, :], h_bf16[:, g, t, :], ident_bf16[:])
+            h_T.append(h_T_bank)
+        nc.vector.tensor_copy(out=h_grouped[:, 0], in_=h_T[0][:].rearrange("p t b -> p b t"))
+        nc.scalar.copy(out=h_grouped[:, 1], in_=h_T[1][:].rearrange("p t b -> p b t"))
+        for g in range(H_PASSES):
+            nc.vector.quantize_mx(
+                out=h_codes[:, g, :].bitcast(FP8X4),
+                scales=h_scales[:, g, :],
+                in_=h_grouped[:, g].rearrange("p b t -> p (b t)"),
+            )
+        sum_h_squares(1)
+        h_norm = keep.tile([P, 1], F32)
+        nc.vector.tensor_add(out=h_norm[:], in0=h_norm_parts[:, 0:1], in1=h_norm_parts[:, 1:2])
+        floor = keep.tile([P, 1], F32)
+        nc.vector.tensor_scalar(out=floor[:], in0=h_norm[:], scalar1=-1.0, scalar2=1.0, op0=ALU.mult, op1=ALU.add)
+
+        clamped = large.tile([P, Y_BANKS, BANK], F32, tag="large")
+        logs = large.tile([P, Y_BANKS, BANK], F32, tag="large")
+        least_parts = keep.tile([P, Y_BANKS], F32)
+        for T in range(Y_BANKS):
+            cross = banks.tile([P, BANK], F32, tag="bank")
+            for g in range(H_PASSES):
+                nc.tensor.matmul_mx(
+                    out=cross[:],
+                    lhsT=h_codes[:, g, :].bitcast(FP8X4),
+                    lhsT_scale=h_scales[:, g, :],
+                    rhs=wq_codes[:, g, BANK * T : BANK * (T + 1)].bitcast(FP8X4),
+                    rhs_scale=wq_scales[:, g, BANK * T : BANK * (T + 1)],
+                    start=(g == 0),
+                    stop=(g == H_PASSES - 1),
+                )
+            nc.vector.scalar_tensor_tensor(
+                out=clamped[:, T, :].rearrange("b (p s) -> b p s", s=ROWS_PER_PARTITION),
+                in0=cross[:].rearrange("b (s p) -> b p s", s=ROWS_PER_PARTITION),
+                scalar=-2.0,
+                in1=norms_plus_1[:, T, :].rearrange("b (p s) -> b p s", s=ROWS_PER_PARTITION),
+                op0=ALU.mult,
+                op1=ALU.add,
+            )
+            nc.vector.tensor_scalar(
+                out=clamped[:, T, :], in0=clamped[:, T, :], scalar1=floor[:, 0:1], scalar2=None,
+                op0=ALU.max, op1=ALU.min, accum_out=least_parts[:, T : T + 1],
+            )
+            nc.scalar.activation(out=logs[:, T, :], in_=clamped[:, T, :], func=ACT.Ln, bias=h_norm[:, 0:1])
+
+        least = keep.tile([P, 1], F32)
+        nc.vector.tensor_reduce(out=least[:], in_=least_parts[:], axis=AXIS.X, op=ALU.min)
+        least_log = keep.tile([P, 1], F32)
+        nc.scalar.activation(out=least_log[:], in_=least[:], func=ACT.Ln, bias=h_norm[:, 0:1])
+        terms = large.tile([P, NY], F32, tag="large")
+        total = keep.tile([P, 1], F32)
+        nc.scalar.activation(
+            out=terms[:], in_=logs[:].rearrange("b T j -> b (T j)"), func=ACT.Exp, scale=-1.0, bias=least_log[:, 0:1],
+            accum_out=total[:],
+        )
+        log_total = keep.tile([P, 1], F32)
+        nc.scalar.activation(out=log_total[:], in_=total[:], func=ACT.Ln)
+        shift = keep.tile([P, 1], F32)
+        nc.vector.tensor_sub(out=shift[:], in0=least_log[:], in1=log_total[:])
+        result = large.tile([P, Y_BANKS, BANK], F32, tag="large")
+        for T in range(Y_BANKS):
+            if T % 2 == 0:
+                nc.vector.tensor_scalar(
+                    out=result[:, T, :], in0=logs[:, T, :], scalar1=-1.0, scalar2=shift[:, 0:1], op0=ALU.mult, op1=ALU.add
+                )
+            else:
+                nc.scalar.activation(out=result[:, T, :], in_=logs[:, T, :], func=ACT.Identity, scale=-1.0, bias=shift[:, 0:1])
+            nc.sync.dma_start(out=out[:, BANK * T : BANK * (T + 1)], in_=result[:, T, :])

@@ -70,13 +70,13 @@ def tile_tnet_k_kernel(tc, x, W_fc_words, W_fc_scales, b_fc, W_q, out):
             nc.sync.dma_start(out=x_chunk[:], in_=x[:, SLOT * c : SLOT * (c + 1)])
             x_chunks.append(x_chunk)
 
-        scale_rows = W_fc_scales.bitcast(I32).rearrange("(a i) q n -> q i a n", i=PLANES_PER_TILE)
-        planes_i32 = w_planes[:].bitcast(I32)
+        scale_rows = W_fc_scales.bitcast(F32).rearrange("(a i) q n -> q i a n", i=PLANES_PER_TILE)
+        planes_f32 = w_planes[:].bitcast(F32)
         for quadrant in range(4):
             for r in range(4):
                 first = 32 * quadrant + r
-                nc.sync.dma_start(
-                    out=planes_i32[first : first + 4 * PLANES_PER_TILE : 4],
+                nc.gpsimd.dma_start(
+                    out=planes_f32[first : first + 4 * PLANES_PER_TILE : 4],
                     in_=scale_rows[4 * quadrant + r],
                 )
 

@@ -30,11 +30,11 @@ SLOT = 4096
 X_CHUNKS = NX // SLOT
 TILE_UNITS = 4
 ROWS_PER_PARTITION = 4
-W_CHUNK_PASSES = 2
-W_CHUNKS = X_PASSES // W_CHUNK_PASSES
+W_LOADS = [(g, 2) for g in range(0, X_PASSES - 2, 2)] + [(X_PASSES - 2, 1), (X_PASSES - 1, 1)]
 W_BUFFERS = 8
 PLANES_PER_TILE = 4
-NORMS_AFTER_CHUNK = 3 * W_CHUNKS // 4
+NORMS_AFTER_LOAD = 3 * len(W_LOADS) // 4
+LOGS_BEFORE_TOTAL = 2
 
 FLOPS = 2 * P * NX * NH + 2 * P * NH * NY
 
@@ -59,10 +59,8 @@ def tile_tnet_k_kernel(tc, x, W_fc_words, W_fc_scales, b_fc, W_q, out):
         nc.scalar.dma_start(out=bias_rows[0:1, :], in_=b_fc.rearrange("(o n) -> o n", o=1))
         ident_f32 = keep.tile([P, P], F32)
         make_identity(nc, ident_f32[:])
-        ident_bf16 = keep.tile([P, P], BF16)
-        make_identity(nc, ident_bf16[:])
         warm = keep.tile([P, 1], F32)
-        nc.scalar.activation(out=warm[:], in_=ones[:, 0:1], func=ACT.Ln)
+        nc.scalar.activation(out=warm[:], in_=ones[:, 0:1], func=ACT.Abs_reciprocal_sqrt)
 
         x_chunks = []
         for c in range(X_CHUNKS):
@@ -70,13 +68,13 @@ def tile_tnet_k_kernel(tc, x, W_fc_words, W_fc_scales, b_fc, W_q, out):
             nc.sync.dma_start(out=x_chunk[:], in_=x[:, SLOT * c : SLOT * (c + 1)])
             x_chunks.append(x_chunk)
 
-        scale_rows = W_fc_scales.bitcast(F32).rearrange("(a i) q n -> q i a n", i=PLANES_PER_TILE)
-        planes_f32 = w_planes[:].bitcast(F32)
+        scale_rows = W_fc_scales.bitcast(I32).rearrange("(a i) q n -> q i a n", i=PLANES_PER_TILE)
+        planes_i32 = w_planes[:].bitcast(I32)
         for quadrant in range(4):
             for r in range(4):
                 first = 32 * quadrant + r
-                nc.gpsimd.dma_start(
-                    out=planes_f32[first : first + 4 * PLANES_PER_TILE : 4],
+                nc.sync.dma_start(
+                    out=planes_i32[first : first + 4 * PLANES_PER_TILE : 4],
                     in_=scale_rows[4 * quadrant + r],
                 )
 
@@ -93,11 +91,9 @@ def tile_tnet_k_kernel(tc, x, W_fc_words, W_fc_scales, b_fc, W_q, out):
         w_chunks = []
 
         def load_w_chunk(c):
-            w_chunk = stream.tile([P, W_CHUNK_PASSES, NH], U32, tag="w_chunk", name="w_chunk%d" % c, align_bytes=64)
-            nc.sync.dma_start(
-                out=w_chunk[:].bitcast(I32),
-                in_=w_words_dram[:, W_CHUNK_PASSES * c : W_CHUNK_PASSES * (c + 1), :],
-            )
+            first, passes = W_LOADS[c]
+            w_chunk = stream.tile([P, passes, NH], U32, tag="w_chunk", name="w_chunk%d" % c, align_bytes=64)
+            nc.sync.dma_start(out=w_chunk[:].bitcast(I32), in_=w_words_dram[:, first : first + passes, :])
             w_chunks.append(w_chunk)
 
         for c in range(W_BUFFERS):
@@ -173,9 +169,9 @@ def tile_tnet_k_kernel(tc, x, W_fc_words, W_fc_scales, b_fc, W_q, out):
 
         h_acc = [h_banks.tile([P, BANK], F32, name="h_acc%d" % n) for n in range(H_PASSES)]
         norms_plus_1 = None
-        for c in range(W_CHUNKS):
-            for i in range(W_CHUNK_PASSES):
-                g = W_CHUNK_PASSES * c + i
+        for c, (first, passes) in enumerate(W_LOADS):
+            for i in range(passes):
+                g = first + i
                 plane_start = 4 * (g % PLANES_PER_TILE)
                 for n in range(H_PASSES):
                     columns = slice(BANK * n, BANK * (n + 1))
@@ -188,10 +184,10 @@ def tile_tnet_k_kernel(tc, x, W_fc_words, W_fc_scales, b_fc, W_q, out):
                         start=(g == 0),
                         stop=(g == X_PASSES - 1),
                     )
-            if c + W_BUFFERS < W_CHUNKS:
+            if c + W_BUFFERS < len(W_LOADS):
                 load_w_chunk(c + W_BUFFERS)
 
-            if c == NORMS_AFTER_CHUNK:
+            if c == NORMS_AFTER_LOAD:
                 norms_plus_1 = large.tile([P, Y_BANKS, BANK], F32, tag="large")
                 for T in range(Y_BANKS):
                     norm_bank = banks.tile([P, ROWS_PER_PARTITION, P], F32, tag="bank")
@@ -207,7 +203,6 @@ def tile_tnet_k_kernel(tc, x, W_fc_words, W_fc_scales, b_fc, W_q, out):
                     )
 
         pre = keep.tile([P, H_PASSES, PACK, P], F32)
-        h_bf16 = keep.tile([P, H_PASSES, PACK, P], BF16)
         h_squares = keep.tile([P, H_PASSES, K_PASS], F32)
         h_norm_parts = keep.tile([P, H_PASSES], F32)
         h_grouped = keep.tile([P, H_PASSES, P, PACK], BF16, align_bytes=64)
@@ -225,16 +220,12 @@ def tile_tnet_k_kernel(tc, x, W_fc_words, W_fc_scales, b_fc, W_q, out):
             nc.vector.tensor_tensor(
                 out=pre[:, g], in0=h_acc[g][:].rearrange("b (p t) -> b t p", t=PACK), in1=bias_sorted[:, g], op=ALU.add
             )
-            nc.scalar.activation(out=h_bf16[:, g], in_=pre[:, g], func=ACT.Relu)
-        sum_h_squares(0)
-        h_T = []
         for g in range(H_PASSES):
-            h_T_bank = banks.tile([P, PACK, P], BF16, tag="bank", name="h_T_bank%d" % g)
+            pre_T = banks.tile([P, PACK, P], F32, tag="bank")
             for t in range(PACK):
-                nc.tensor.transpose(h_T_bank[:, t, :], h_bf16[:, g, t, :], ident_bf16[:])
-            h_T.append(h_T_bank)
-        nc.vector.tensor_copy(out=h_grouped[:, 0], in_=h_T[0][:].rearrange("p t b -> p b t"))
-        nc.scalar.copy(out=h_grouped[:, 1], in_=h_T[1][:].rearrange("p t b -> p b t"))
+                nc.tensor.transpose(pre_T[:, t, :], pre[:, g, t, :], ident_f32[:])
+            nc.scalar.activation(out=h_grouped[:, g], in_=pre_T[:].rearrange("p t b -> p b t"), func=ACT.Relu)
+        sum_h_squares(0)
         for g in range(H_PASSES):
             nc.vector.quantize_mx(
                 out=h_codes[:, g, :].bitcast(FP8X4),
@@ -248,7 +239,7 @@ def tile_tnet_k_kernel(tc, x, W_fc_words, W_fc_scales, b_fc, W_q, out):
         nc.vector.tensor_scalar(out=floor[:], in0=h_norm[:], scalar1=-1.0, scalar2=1.0, op0=ALU.mult, op1=ALU.add)
 
         clamped = large.tile([P, Y_BANKS, BANK], F32, tag="large")
-        logs = large.tile([P, Y_BANKS, BANK], F32, tag="large")
+        roots = large.tile([P, Y_BANKS, BANK], F32, tag="large")
         least_parts = keep.tile([P, Y_BANKS], F32)
         for T in range(Y_BANKS):
             cross = banks.tile([P, BANK], F32, tag="bank")
@@ -274,28 +265,39 @@ def tile_tnet_k_kernel(tc, x, W_fc_words, W_fc_scales, b_fc, W_q, out):
                 out=clamped[:, T, :], in0=clamped[:, T, :], scalar1=floor[:, 0:1], scalar2=None,
                 op0=ALU.max, op1=ALU.min, accum_out=least_parts[:, T : T + 1],
             )
-            nc.scalar.activation(out=logs[:, T, :], in_=clamped[:, T, :], func=ACT.Ln, bias=h_norm[:, 0:1])
+            nc.scalar.activation(
+                out=roots[:, T, :], in_=clamped[:, T, :], func=ACT.Abs_reciprocal_sqrt, bias=h_norm[:, 0:1]
+            )
 
         least = keep.tile([P, 1], F32)
         nc.vector.tensor_reduce(out=least[:], in_=least_parts[:], axis=AXIS.X, op=ALU.min)
-        least_log = keep.tile([P, 1], F32)
-        nc.scalar.activation(out=least_log[:], in_=least[:], func=ACT.Ln, bias=h_norm[:, 0:1])
+        top_root = keep.tile([P, 1], F32)
+        nc.scalar.activation(out=top_root[:], in_=least[:], func=ACT.Abs_reciprocal_sqrt, bias=h_norm[:, 0:1])
+        inverse_top = keep.tile([P, 1], F32)
+        nc.vector.reciprocal(out=inverse_top[:], in_=top_root[:])
         terms = large.tile([P, NY], F32, tag="large")
-        total = keep.tile([P, 1], F32)
-        nc.scalar.activation(
-            out=terms[:], in_=logs[:].rearrange("b T j -> b (T j)"), func=ACT.Exp, scale=-1.0, bias=least_log[:, 0:1],
-            accum_out=total[:],
+        terms_sum = keep.tile([P, 1], F32)
+        roots_flat = roots[:].rearrange("b T j -> b (T j)")
+        nc.vector.scalar_tensor_tensor(
+            out=terms[:], in0=roots_flat, scalar=inverse_top[:, 0:1], in1=roots_flat, op0=ALU.mult, op1=ALU.mult,
+            accum_out=terms_sum[:],
         )
+        total = keep.tile([P, 1], F32)
+        nc.vector.tensor_mul(out=total[:], in0=terms_sum[:], in1=inverse_top[:])
+
+        logs = large.tile([P, Y_BANKS, BANK], F32, tag="large")
+        least_log = keep.tile([P, 1], F32)
         log_total = keep.tile([P, 1], F32)
-        nc.scalar.activation(out=log_total[:], in_=total[:], func=ACT.Ln)
         shift = keep.tile([P, 1], F32)
-        nc.vector.tensor_sub(out=shift[:], in0=least_log[:], in1=log_total[:])
         result = large.tile([P, Y_BANKS, BANK], F32, tag="large")
+        nc.scalar.activation(out=least_log[:], in_=least[:], func=ACT.Ln, bias=h_norm[:, 0:1])
         for T in range(Y_BANKS):
-            if T % 2 == 0:
-                nc.vector.tensor_scalar(
-                    out=result[:, T, :], in0=logs[:, T, :], scalar1=-1.0, scalar2=shift[:, 0:1], op0=ALU.mult, op1=ALU.add
-                )
-            else:
-                nc.scalar.activation(out=result[:, T, :], in_=logs[:, T, :], func=ACT.Identity, scale=-1.0, bias=shift[:, 0:1])
+            if T == LOGS_BEFORE_TOTAL:
+                nc.scalar.activation(out=log_total[:], in_=total[:], func=ACT.Ln)
+                nc.vector.tensor_sub(out=shift[:], in0=least_log[:], in1=log_total[:])
+            nc.scalar.activation(out=logs[:, T, :], in_=clamped[:, T, :], func=ACT.Ln, bias=h_norm[:, 0:1])
+        for T in range(Y_BANKS):
+            nc.vector.tensor_scalar(
+                out=result[:, T, :], in0=logs[:, T, :], scalar1=-1.0, scalar2=shift[:, 0:1], op0=ALU.mult, op1=ALU.add
+            )
             nc.sync.dma_start(out=out[:, BANK * T : BANK * (T + 1)], in_=result[:, T, :])

@@ -30,11 +30,19 @@ SLOT = 4096
 X_CHUNKS = NX // SLOT
 TILE_UNITS = 4
 ROWS_PER_PARTITION = 4
-W_LOADS = [(g, 2) for g in range(0, X_PASSES - 2, 2)] + [(X_PASSES - 2, 1), (X_PASSES - 1, 1)]
+SPLIT_PASSES = 6
+W_LOADS = (
+    [(g, 2, (0, 1)) for g in range(0, X_PASSES - SPLIT_PASSES, 2)]
+    + [(g, 2, (0,)) for g in range(X_PASSES - SPLIT_PASSES, X_PASSES, 2)]
+    + [(g, 2, (1,)) for g in range(X_PASSES - SPLIT_PASSES, X_PASSES - 2, 2)]
+    + [(X_PASSES - 2, 1, (1,)), (X_PASSES - 1, 1, (1,))]
+)
 W_BUFFERS = 8
 PLANES_PER_TILE = 4
-NORMS_AFTER_LOAD = 3 * len(W_LOADS) // 4
-LOGS_BEFORE_TOTAL = 2
+NORMS_AFTER_LOAD = (X_PASSES - SPLIT_PASSES) // 2 - 4
+VECTOR_BANKS = (0, 1)
+GPSIMD_BANKS = (2, 3)
+LOGS_BEFORE_TOTAL = 1
 
 FLOPS = 2 * P * NX * NH + 2 * P * NH * NY
 
@@ -56,7 +64,6 @@ def tile_tnet_k_kernel(tc, x, W_fc_words, W_fc_scales, b_fc, W_q, out):
         nc.vector.memset(ones[:], 1.0)
         bias_rows = keep.tile([P, NH], BF16)
         nc.vector.memset(bias_rows[:], 0.0)
-        nc.scalar.dma_start(out=bias_rows[0:1, :], in_=b_fc.rearrange("(o n) -> o n", o=1))
         ident_f32 = keep.tile([P, P], F32)
         make_identity(nc, ident_f32[:])
         warm = keep.tile([P, 1], F32)
@@ -86,14 +93,16 @@ def tile_tnet_k_kernel(tc, x, W_fc_words, W_fc_scales, b_fc, W_q, out):
                 in_=W_q[BANK * T : BANK * (T + 1), :].rearrange("(p s) k -> p s k", s=ROWS_PER_PARTITION),
             )
             wq_chunks.append(wq_chunk)
+        nc.sync.dma_start(out=bias_rows[0:1, :], in_=b_fc.rearrange("(o n) -> o n", o=1))
 
         w_words_dram = W_fc_words.rearrange("g p n t -> p g (n t)").bitcast(I32)
         w_chunks = []
 
         def load_w_chunk(c):
-            first, passes = W_LOADS[c]
-            w_chunk = stream.tile([P, passes, NH], U32, tag="w_chunk", name="w_chunk%d" % c, align_bytes=64)
-            nc.sync.dma_start(out=w_chunk[:].bitcast(I32), in_=w_words_dram[:, first : first + passes, :])
+            first, passes, halves = W_LOADS[c]
+            columns = slice(BANK * halves[0], BANK * (halves[-1] + 1))
+            w_chunk = stream.tile([P, passes, BANK * len(halves)], U32, tag="w_chunk", name="w_chunk%d" % c, align_bytes=64)
+            nc.sync.dma_start(out=w_chunk[:].bitcast(I32), in_=w_words_dram[:, first : first + passes, columns])
             w_chunks.append(w_chunk)
 
         for c in range(W_BUFFERS):
@@ -163,29 +172,68 @@ def tile_tnet_k_kernel(tc, x, W_fc_words, W_fc_scales, b_fc, W_q, out):
             for s in range(ROWS_PER_PARTITION):
                 squares = stage.tile([P, NH], BF16, tag="squares")
                 column = ROWS_PER_PARTITION * T + s
-                nc.scalar.activation(
-                    out=squares[:], in_=wq_chunks[T][:, s, :], func=ACT.Square, accum_out=wq_norms[:, column : column + 1]
-                )
+                row = wq_chunks[T][:, s, :]
+                if s % 2 == 0:
+                    nc.scalar.activation(
+                        out=squares[:], in_=row, func=ACT.Square, accum_out=wq_norms[:, column : column + 1]
+                    )
+                else:
+                    nc.vector.scalar_tensor_tensor(
+                        out=squares[:], in0=row, scalar=1.0, in1=row, op0=ALU.mult, op1=ALU.mult,
+                        accum_out=wq_norms[:, column : column + 1],
+                    )
+
+        pre = keep.tile([P, H_PASSES, PACK, P], F32)
+        h_squares = keep.tile([P, H_PASSES, K_PASS], F32)
+        h_norm_parts = keep.tile([P, H_PASSES], F32)
+        h_grouped = keep.tile([P, H_PASSES, P, PACK], BF16, align_bytes=64)
+        h_codes = keep.tile([P, H_PASSES, P], U32, align_bytes=64)
+        h_scales = keep.tile([P, H_PASSES, P], U8, align_bytes=64)
+
+        def add_bias(g):
+            nc.vector.tensor_tensor(
+                out=pre[:, g], in0=h_acc[g][:].rearrange("b (p t) -> b t p", t=PACK), in1=bias_sorted[:, g], op=ALU.add
+            )
+            flat = pre[:, g].rearrange("b t p -> b (t p)")
+            nc.vector.scalar_tensor_tensor(
+                out=h_squares[:, g, :], in0=flat, scalar=0.0, in1=flat, op0=ALU.max, op1=ALU.mult,
+                accum_out=h_norm_parts[:, g : g + 1],
+            )
+
+        def transpose_half(g):
+            pre_T = banks.tile([P, PACK, P], F32, tag="bank")
+            for t in range(PACK):
+                nc.tensor.transpose(pre_T[:, t, :], pre[:, g, t, :], ident_f32[:])
+            nc.scalar.activation(out=h_grouped[:, g], in_=pre_T[:].rearrange("p t b -> p b t"), func=ACT.Relu)
+            nc.vector.quantize_mx(
+                out=h_codes[:, g, :].bitcast(FP8X4),
+                scales=h_scales[:, g, :],
+                in_=h_grouped[:, g].rearrange("p b t -> p (b t)"),
+            )
 
         h_acc = [h_banks.tile([P, BANK], F32, name="h_acc%d" % n) for n in range(H_PASSES)]
         norms_plus_1 = None
-        for c, (first, passes) in enumerate(W_LOADS):
+        for c, (first, passes, halves) in enumerate(W_LOADS):
             for i in range(passes):
                 g = first + i
                 plane_start = 4 * (g % PLANES_PER_TILE)
-                for n in range(H_PASSES):
-                    columns = slice(BANK * n, BANK * (n + 1))
+                for n in halves:
+                    start = BANK * (n - halves[0])
                     nc.tensor.matmul_mx(
                         out=h_acc[n][:],
                         lhsT=a_codes[:, g, :].bitcast(FP8X4),
                         lhsT_scale=a_scales[:, g, :],
-                        rhs=w_chunks[c][:, i, columns].bitcast(FP8X4),
-                        rhs_scale=w_planes[plane_start:P, g // PLANES_PER_TILE, columns],
+                        rhs=w_chunks[c][:, i, start : start + BANK].bitcast(FP8X4),
+                        rhs_scale=w_planes[plane_start:P, g // PLANES_PER_TILE, BANK * n : BANK * (n + 1)],
                         start=(g == 0),
                         stop=(g == X_PASSES - 1),
                     )
+                if g == X_PASSES - 1:
+                    add_bias(halves[-1])
             if c + W_BUFFERS < len(W_LOADS):
                 load_w_chunk(c + W_BUFFERS)
+            if first == X_PASSES - SPLIT_PASSES and halves == (1,):
+                transpose_half(0)
 
             if c == NORMS_AFTER_LOAD:
                 norms_plus_1 = large.tile([P, Y_BANKS, BANK], F32, tag="large")
@@ -202,65 +250,39 @@ def tile_tnet_k_kernel(tc, x, W_fc_words, W_fc_scales, b_fc, W_q, out):
                         scalar1=1.0,
                     )
 
-        pre = keep.tile([P, H_PASSES, PACK, P], F32)
-        h_squares = keep.tile([P, H_PASSES, K_PASS], F32)
-        h_norm_parts = keep.tile([P, H_PASSES], F32)
-        h_grouped = keep.tile([P, H_PASSES, P, PACK], BF16, align_bytes=64)
-        h_codes = keep.tile([P, H_PASSES, P], U32, align_bytes=64)
-        h_scales = keep.tile([P, H_PASSES, P], U8, align_bytes=64)
+        crosses = [banks.tile([P, BANK], F32, tag="bank", name="cross%d" % T) for T in range(Y_BANKS)]
 
-        def sum_h_squares(g):
-            flat = pre[:, g].rearrange("b t p -> b (t p)")
-            nc.vector.scalar_tensor_tensor(
-                out=h_squares[:, g, :], in0=flat, scalar=0.0, in1=flat, op0=ALU.max, op1=ALU.mult,
-                accum_out=h_norm_parts[:, g : g + 1],
+        def multiply_half(g, T):
+            nc.tensor.matmul_mx(
+                out=crosses[T][:],
+                lhsT=h_codes[:, g, :].bitcast(FP8X4),
+                lhsT_scale=h_scales[:, g, :],
+                rhs=wq_codes[:, g, BANK * T : BANK * (T + 1)].bitcast(FP8X4),
+                rhs_scale=wq_scales[:, g, BANK * T : BANK * (T + 1)],
+                start=(g == 0),
+                stop=(g == H_PASSES - 1),
             )
 
-        for g in range(H_PASSES):
-            nc.vector.tensor_tensor(
-                out=pre[:, g], in0=h_acc[g][:].rearrange("b (p t) -> b t p", t=PACK), in1=bias_sorted[:, g], op=ALU.add
-            )
-        for g in range(H_PASSES):
-            pre_T = banks.tile([P, PACK, P], F32, tag="bank")
-            for t in range(PACK):
-                nc.tensor.transpose(pre_T[:, t, :], pre[:, g, t, :], ident_f32[:])
-            nc.scalar.activation(out=h_grouped[:, g], in_=pre_T[:].rearrange("p t b -> p b t"), func=ACT.Relu)
-        sum_h_squares(0)
-        for g in range(H_PASSES):
-            nc.vector.quantize_mx(
-                out=h_codes[:, g, :].bitcast(FP8X4),
-                scales=h_scales[:, g, :],
-                in_=h_grouped[:, g].rearrange("p b t -> p (b t)"),
-            )
-        sum_h_squares(1)
         h_norm = keep.tile([P, 1], F32)
         nc.vector.tensor_add(out=h_norm[:], in0=h_norm_parts[:, 0:1], in1=h_norm_parts[:, 1:2])
         floor = keep.tile([P, 1], F32)
         nc.vector.tensor_scalar(out=floor[:], in0=h_norm[:], scalar1=-1.0, scalar2=1.0, op0=ALU.mult, op1=ALU.add)
+        transpose_half(1)
+        for T in range(Y_BANKS):
+            multiply_half(0, T)
 
         clamped = large.tile([P, Y_BANKS, BANK], F32, tag="large")
+        products = large.tile([P, len(GPSIMD_BANKS), BANK], F32, tag="large")
         roots = large.tile([P, Y_BANKS, BANK], F32, tag="large")
         least_parts = keep.tile([P, Y_BANKS], F32)
-        for T in range(Y_BANKS):
-            cross = banks.tile([P, BANK], F32, tag="bank")
-            for g in range(H_PASSES):
-                nc.tensor.matmul_mx(
-                    out=cross[:],
-                    lhsT=h_codes[:, g, :].bitcast(FP8X4),
-                    lhsT_scale=h_scales[:, g, :],
-                    rhs=wq_codes[:, g, BANK * T : BANK * (T + 1)].bitcast(FP8X4),
-                    rhs_scale=wq_scales[:, g, BANK * T : BANK * (T + 1)],
-                    start=(g == 0),
-                    stop=(g == H_PASSES - 1),
-                )
-            nc.vector.scalar_tensor_tensor(
-                out=clamped[:, T, :].rearrange("b (p s) -> b p s", s=ROWS_PER_PARTITION),
-                in0=cross[:].rearrange("b (s p) -> b p s", s=ROWS_PER_PARTITION),
-                scalar=-2.0,
-                in1=norms_plus_1[:, T, :].rearrange("b (p s) -> b p s", s=ROWS_PER_PARTITION),
-                op0=ALU.mult,
-                op1=ALU.add,
-            )
+
+        def by_row_group(bank):
+            return bank.rearrange("b (s p) -> b p s", s=ROWS_PER_PARTITION)
+
+        def by_prototype(bank):
+            return bank.rearrange("b (p s) -> b p s", s=ROWS_PER_PARTITION)
+
+        def clamp_and_root(T):
             nc.vector.tensor_scalar(
                 out=clamped[:, T, :], in0=clamped[:, T, :], scalar1=floor[:, 0:1], scalar2=None,
                 op0=ALU.max, op1=ALU.min, accum_out=least_parts[:, T : T + 1],
@@ -269,30 +291,47 @@ def tile_tnet_k_kernel(tc, x, W_fc_words, W_fc_scales, b_fc, W_q, out):
                 out=roots[:, T, :], in_=clamped[:, T, :], func=ACT.Abs_reciprocal_sqrt, bias=h_norm[:, 0:1]
             )
 
+        for i, T in enumerate(GPSIMD_BANKS):
+            multiply_half(1, T)
+            nc.scalar.activation(
+                out=by_prototype(products[:, i, :]), in_=by_row_group(crosses[T][:]), func=ACT.Copy, scale=-2.0
+            )
+            nc.gpsimd.tensor_tensor(
+                out=clamped[:, T, :], in0=products[:, i, :], in1=norms_plus_1[:, T, :], op=ALU.add
+            )
+        for T in VECTOR_BANKS:
+            multiply_half(1, T)
+            nc.vector.scalar_tensor_tensor(
+                out=by_prototype(clamped[:, T, :]), in0=by_row_group(crosses[T][:]), scalar=-2.0,
+                in1=by_prototype(norms_plus_1[:, T, :]), op0=ALU.mult, op1=ALU.add,
+            )
+            clamp_and_root(T)
+        for T in GPSIMD_BANKS:
+            clamp_and_root(T)
+
+        least_clamped = keep.tile([P, 1], F32)
         least = keep.tile([P, 1], F32)
-        nc.vector.tensor_reduce(out=least[:], in_=least_parts[:], axis=AXIS.X, op=ALU.min)
-        top_root = keep.tile([P, 1], F32)
-        nc.scalar.activation(out=top_root[:], in_=least[:], func=ACT.Abs_reciprocal_sqrt, bias=h_norm[:, 0:1])
-        inverse_top = keep.tile([P, 1], F32)
-        nc.vector.reciprocal(out=inverse_top[:], in_=top_root[:])
+        nc.vector.tensor_reduce(out=least_clamped[:], in_=least_parts[:], axis=AXIS.X, op=ALU.min)
+        nc.vector.tensor_add(out=least[:], in0=least_clamped[:], in1=h_norm[:])
         terms = large.tile([P, NY], F32, tag="large")
-        terms_sum = keep.tile([P, 1], F32)
-        roots_flat = roots[:].rearrange("b T j -> b (T j)")
-        nc.vector.scalar_tensor_tensor(
-            out=terms[:], in0=roots_flat, scalar=inverse_top[:, 0:1], in1=roots_flat, op0=ALU.mult, op1=ALU.mult,
-            accum_out=terms_sum[:],
-        )
+        total_parts = keep.tile([P, 2], F32)
         total = keep.tile([P, 1], F32)
-        nc.vector.tensor_mul(out=total[:], in0=terms_sum[:], in1=inverse_top[:])
+        roots_flat = roots[:].rearrange("b T j -> b (T j)")
+        for part, columns in enumerate([slice(0, NY - BANK), slice(NY - BANK, NY)]):
+            nc.vector.scalar_tensor_tensor(
+                out=terms[:, columns], in0=roots_flat[:, columns], scalar=least[:, 0:1], in1=roots_flat[:, columns],
+                op0=ALU.mult, op1=ALU.mult, accum_out=total_parts[:, part : part + 1],
+            )
+        nc.vector.tensor_add(out=total[:], in0=total_parts[:, 0:1], in1=total_parts[:, 1:2])
 
         logs = large.tile([P, Y_BANKS, BANK], F32, tag="large")
         least_log = keep.tile([P, 1], F32)
         log_total = keep.tile([P, 1], F32)
         shift = keep.tile([P, 1], F32)
         result = large.tile([P, Y_BANKS, BANK], F32, tag="large")
-        nc.scalar.activation(out=least_log[:], in_=least[:], func=ACT.Ln, bias=h_norm[:, 0:1])
         for T in range(Y_BANKS):
             if T == LOGS_BEFORE_TOTAL:
+                nc.scalar.activation(out=least_log[:], in_=least[:], func=ACT.Ln)
                 nc.scalar.activation(out=log_total[:], in_=total[:], func=ACT.Ln)
                 nc.vector.tensor_sub(out=shift[:], in0=least_log[:], in1=log_total[:])
             nc.scalar.activation(out=logs[:, T, :], in_=clamped[:, T, :], func=ACT.Ln, bias=h_norm[:, 0:1])

@@ -37,9 +37,10 @@ W_LOADS = (
     + [(g, 2, (1,)) for g in range(X_PASSES - SPLIT_PASSES, X_PASSES - 2, 2)]
     + [(X_PASSES - 2, 1, (1,)), (X_PASSES - 1, 1, (1,))]
 )
+WQ_BEHIND_LOAD = (2, 4, 6, 8)
 W_BUFFERS = 8
 PLANES_PER_TILE = 4
-NORMS_AFTER_LOAD = (X_PASSES - SPLIT_PASSES) // 2 - 4
+NORMS_AFTER_LOAD = (X_PASSES - SPLIT_PASSES) // 2 - 2
 VECTOR_BANKS = (0, 1)
 GPSIMD_BANKS = (2, 3)
 LOGS_BEFORE_TOTAL = 1
@@ -85,18 +86,9 @@ def tile_tnet_k_kernel(tc, x, W_fc_words, W_fc_scales, b_fc, W_q, out):
                     in_=scale_rows[4 * quadrant + r],
                 )
 
-        wq_chunks = []
-        for T in range(Y_BANKS):
-            wq_chunk = large.tile([P, ROWS_PER_PARTITION, NH], BF16, tag="large", name="wq_chunk%d" % T)
-            nc.sync.dma_start(
-                out=wq_chunk[:],
-                in_=W_q[BANK * T : BANK * (T + 1), :].rearrange("(p s) k -> p s k", s=ROWS_PER_PARTITION),
-            )
-            wq_chunks.append(wq_chunk)
         nc.sync.dma_start(out=bias_rows[0:1, :], in_=b_fc.rearrange("(o n) -> o n", o=1))
 
         w_words_dram = W_fc_words.rearrange("g p n t -> p g (n t)").bitcast(I32)
-        w_chunks = []
 
         def load_w_chunk(c):
             first, passes, halves = W_LOADS[c]
@@ -104,7 +96,17 @@ def tile_tnet_k_kernel(tc, x, W_fc_words, W_fc_scales, b_fc, W_q, out):
             w_chunk = stream.tile([P, passes, BANK * len(halves)], U32, tag="w_chunk", name="w_chunk%d" % c, align_bytes=64)
             nc.sync.dma_start(out=w_chunk[:].bitcast(I32), in_=w_words_dram[:, first : first + passes, columns])
             w_chunks.append(w_chunk)
+            if c in WQ_BEHIND_LOAD:
+                T = WQ_BEHIND_LOAD.index(c)
+                wq_chunk = large.tile([P, ROWS_PER_PARTITION, NH], BF16, tag="large", name="wq_chunk%d" % T)
+                nc.sync.dma_start(
+                    out=wq_chunk[:],
+                    in_=W_q[BANK * T : BANK * (T + 1), :].rearrange("(p s) k -> p s k", s=ROWS_PER_PARTITION),
+                )
+                wq_chunks.append(wq_chunk)
 
+        w_chunks = []
+        wq_chunks = []
         for c in range(W_BUFFERS):
             load_w_chunk(c)
 
@@ -147,16 +149,6 @@ def tile_tnet_k_kernel(tc, x, W_fc_words, W_fc_scales, b_fc, W_q, out):
                     a_codes[:, g : g + TILE_UNITS, :].rearrange("p g b -> p (g b)"),
                     a_scales[:, g : g + TILE_UNITS, :].rearrange("p g b -> p (g b)"),
                 )
-        for T in range(Y_BANKS):
-            wq_words = wq_chunks[T][:].bitcast(F32)
-            for g in range(H_PASSES):
-                grouped = regroup([wq_words[:, s, WORDS * g : WORDS * (g + 1)] for s in range(ROWS_PER_PARTITION)])
-                quantise(*waiting)
-                waiting = (
-                    grouped,
-                    wq_codes[:, g, BANK * T : BANK * (T + 1)],
-                    wq_scales[:, g, BANK * T : BANK * (T + 1)],
-                )
         quantise(*waiting)
 
         bias_sorted = keep.tile([P, H_PASSES, PACK, P], F32)
@@ -168,7 +160,15 @@ def tile_tnet_k_kernel(tc, x, W_fc_words, W_fc_scales, b_fc, W_q, out):
             nc.scalar.copy(out=bias_sorted[:, g], in_=bias_bank[:].rearrange("b (p t) -> b t p", t=PACK))
 
         wq_norms = keep.tile([P, Y_BANKS * ROWS_PER_PARTITION], F32)
-        for T in range(Y_BANKS):
+
+        def work_up_wq(T):
+            wq_words = wq_chunks[T][:].bitcast(F32)
+            grouped = [
+                regroup([wq_words[:, s, WORDS * g : WORDS * (g + 1)] for s in range(ROWS_PER_PARTITION)])
+                for g in range(H_PASSES)
+            ]
+            for g in range(H_PASSES):
+                quantise(grouped[g], wq_codes[:, g, BANK * T : BANK * (T + 1)], wq_scales[:, g, BANK * T : BANK * (T + 1)])
             for s in range(ROWS_PER_PARTITION):
                 squares = stage.tile([P, NH], BF16, tag="squares")
                 column = ROWS_PER_PARTITION * T + s
@@ -232,6 +232,8 @@ def tile_tnet_k_kernel(tc, x, W_fc_words, W_fc_scales, b_fc, W_q, out):
                     add_bias(halves[-1])
             if c + W_BUFFERS < len(W_LOADS):
                 load_w_chunk(c + W_BUFFERS)
+            if c in WQ_BEHIND_LOAD:
+                work_up_wq(WQ_BEHIND_LOAD.index(c))
             if first == X_PASSES - SPLIT_PASSES and halves == (1,):
                 transpose_half(0)
 

@@ -43,7 +43,7 @@ PLANES_PER_TILE = 4
 NORMS_AFTER_LOAD = (X_PASSES - SPLIT_PASSES) // 2 - 2
 VECTOR_BANKS = (0, 1)
 GPSIMD_BANKS = (2, 3)
-LOGS_BEFORE_TOTAL = 1
+STORE_WIDTHS = (256, 256, 512, 512, 512)
 
 FLOPS = 2 * P * NX * NH + 2 * P * NH * NY
 
@@ -76,14 +76,13 @@ def tile_tnet_k_kernel(tc, x, W_fc_words, W_fc_scales, b_fc, W_q, out):
             nc.sync.dma_start(out=x_chunk[:], in_=x[:, SLOT * c : SLOT * (c + 1)])
             x_chunks.append(x_chunk)
 
-        scale_rows = W_fc_scales.bitcast(I32).rearrange("(a i) q n -> q i a n", i=PLANES_PER_TILE)
-        planes_i32 = w_planes[:].bitcast(I32)
-        for quadrant in range(4):
-            for r in range(4):
-                first = 32 * quadrant + r
-                nc.sync.dma_start(
-                    out=planes_i32[first : first + 4 * PLANES_PER_TILE : 4],
-                    in_=scale_rows[4 * quadrant + r],
+        planes_words = w_planes[:].bitcast(F32)
+        for a in range(X_PASSES // PLANES_PER_TILE):
+            passes = slice(PLANES_PER_TILE * a, PLANES_PER_TILE * (a + 1))
+            for quadrant in range(4):
+                nc.gpsimd.dma_start(
+                    out=planes_words[32 * quadrant : 32 * quadrant + 16, a, :],
+                    in_=W_fc_scales[passes, 4 * quadrant : 4 * quadrant + 4, :].bitcast(F32),
                 )
 
         nc.sync.dma_start(out=bias_rows[0:1, :], in_=b_fc.rearrange("(o n) -> o n", o=1))
@@ -311,34 +310,34 @@ def tile_tnet_k_kernel(tc, x, W_fc_words, W_fc_scales, b_fc, W_q, out):
         for T in GPSIMD_BANKS:
             clamp_and_root(T)
 
-        least_clamped = keep.tile([P, 1], F32)
+        least_terms = keep.tile([P, Y_BANKS], F32)
         least = keep.tile([P, 1], F32)
-        nc.vector.tensor_reduce(out=least_clamped[:], in_=least_parts[:], axis=AXIS.X, op=ALU.min)
-        nc.vector.tensor_add(out=least[:], in0=least_clamped[:], in1=h_norm[:])
+        nc.vector.tensor_scalar(
+            out=least_terms[:], in0=least_parts[:], scalar1=h_norm[:, 0:1], scalar2=None,
+            op0=ALU.add, op1=ALU.min, accum_out=least[:],
+        )
         terms = large.tile([P, NY], F32, tag="large")
         total_parts = keep.tile([P, 2], F32)
-        total = keep.tile([P, 1], F32)
         roots_flat = roots[:].rearrange("b T j -> b (T j)")
         for part, columns in enumerate([slice(0, NY - BANK), slice(NY - BANK, NY)]):
             nc.vector.scalar_tensor_tensor(
                 out=terms[:, columns], in0=roots_flat[:, columns], scalar=least[:, 0:1], in1=roots_flat[:, columns],
                 op0=ALU.mult, op1=ALU.mult, accum_out=total_parts[:, part : part + 1],
             )
-        nc.vector.tensor_add(out=total[:], in0=total_parts[:, 0:1], in1=total_parts[:, 1:2])
 
-        logs = large.tile([P, Y_BANKS, BANK], F32, tag="large")
-        least_log = keep.tile([P, 1], F32)
+        logs = large.tile([P, NY], F32, tag="large")
         log_total = keep.tile([P, 1], F32)
-        shift = keep.tile([P, 1], F32)
-        result = large.tile([P, Y_BANKS, BANK], F32, tag="large")
         for T in range(Y_BANKS):
-            if T == LOGS_BEFORE_TOTAL:
-                nc.scalar.activation(out=least_log[:], in_=least[:], func=ACT.Ln)
-                nc.scalar.activation(out=log_total[:], in_=total[:], func=ACT.Ln)
-                nc.vector.tensor_sub(out=shift[:], in0=least_log[:], in1=log_total[:])
-            nc.scalar.activation(out=logs[:, T, :], in_=clamped[:, T, :], func=ACT.Ln, bias=h_norm[:, 0:1])
-        for T in range(Y_BANKS):
-            nc.vector.tensor_scalar(
-                out=result[:, T, :], in0=logs[:, T, :], scalar1=-1.0, scalar2=shift[:, 0:1], op0=ALU.mult, op1=ALU.add
-            )
-            nc.sync.dma_start(out=out[:, BANK * T : BANK * (T + 1)], in_=result[:, T, :])
+            columns = slice(BANK * T, BANK * (T + 1))
+            nc.scalar.activation(out=logs[:, columns], in_=terms[:, columns], func=ACT.Ln)
+            if T == 0:
+                nc.scalar.activation(
+                    out=log_total[:], in_=total_parts[:, 0:1], func=ACT.Ln, bias=total_parts[:, 1:2]
+                )
+        result = large.tile([P, NY], F32, tag="large")
+        first = 0
+        for width in STORE_WIDTHS:
+            columns = slice(first, first + width)
+            nc.vector.tensor_scalar_sub(out=result[:, columns], in0=logs[:, columns], scalar1=log_total[:, 0:1])
+            nc.sync.dma_start(out=out[:, columns], in_=result[:, columns])
+            first += width

@@ -185,6 +185,7 @@ def tile_tnet_k_kernel(tc, x, W_fc_words, W_fc_scales, b_fc, W_q, out):
         pre = keep.tile([P, H_PASSES, PACK, P], F32)
         h_squares = keep.tile([P, H_PASSES, K_PASS], F32)
         h_norm_parts = keep.tile([P, H_PASSES], F32)
+        floor_part = keep.tile([P, 1], F32)
         h_grouped = keep.tile([P, H_PASSES, P, PACK], BF16, align_bytes=64)
         h_codes = keep.tile([P, H_PASSES, P], U32, align_bytes=64)
         h_scales = keep.tile([P, H_PASSES, P], U8, align_bytes=64)
@@ -198,12 +199,22 @@ def tile_tnet_k_kernel(tc, x, W_fc_words, W_fc_scales, b_fc, W_q, out):
                 out=h_squares[:, g, :], in0=flat, scalar=0.0, in1=flat, op0=ALU.max, op1=ALU.mult,
                 accum_out=h_norm_parts[:, g : g + 1],
             )
+            if g == 0:
+                nc.vector.tensor_scalar(
+                    out=floor_part[:], in0=h_norm_parts[:, 0:1], scalar1=-1.0, scalar2=1.0, op0=ALU.mult, op1=ALU.add
+                )
 
         def transpose_half(g):
-            pre_T = banks.tile([P, PACK, P], F32, tag="bank")
-            for t in range(PACK):
-                nc.tensor.transpose(pre_T[:, t, :], pre[:, g, t, :], ident_f32[:])
-            nc.scalar.activation(out=h_grouped[:, g], in_=pre_T[:].rearrange("p t b -> p b t"), func=ACT.Relu)
+            for first in range(0, PACK, 2):
+                pre_T = banks.tile([P, 2, P], F32, tag="bank")
+                for i in range(2):
+                    nc.tensor.transpose(pre_T[:, i, :], pre[:, g, first + i, :], ident_f32[:])
+                target = h_grouped[:, g, :, first : first + 2]
+                source = pre_T[:].rearrange("p t b -> p b t")
+                if first == 0:
+                    nc.scalar.activation(out=target, in_=source, func=ACT.Relu)
+                else:
+                    nc.vector.tensor_scalar_max(out=target, in0=source, scalar1=0.0)
             nc.vector.quantize_mx(
                 out=h_codes[:, g, :].bitcast(FP8X4),
                 scales=h_scales[:, g, :],
@@ -264,18 +275,20 @@ def tile_tnet_k_kernel(tc, x, W_fc_words, W_fc_scales, b_fc, W_q, out):
                 stop=(g == H_PASSES - 1),
             )
 
+        bank_order = [T for pair in zip(GPSIMD_BANKS, VECTOR_BANKS) for T in pair]
+        for T in bank_order[:-1]:
+            multiply_half(0, T)
+        transpose_half(1)
         h_norm = keep.tile([P, 1], F32)
         nc.vector.tensor_add(out=h_norm[:], in0=h_norm_parts[:, 0:1], in1=h_norm_parts[:, 1:2])
         floor = keep.tile([P, 1], F32)
-        nc.vector.tensor_scalar(out=floor[:], in0=h_norm[:], scalar1=-1.0, scalar2=1.0, op0=ALU.mult, op1=ALU.add)
-        transpose_half(1)
-        for T in range(Y_BANKS):
-            multiply_half(0, T)
+        nc.vector.tensor_sub(out=floor[:], in0=floor_part[:], in1=h_norm_parts[:, 1:2])
+        multiply_half(0, bank_order[-1])
 
         clamped = large.tile([P, Y_BANKS, BANK], F32, tag="large")
         products = large.tile([P, len(GPSIMD_BANKS), BANK], F32, tag="large")
         roots = large.tile([P, Y_BANKS, BANK], F32, tag="large")
-        least_parts = keep.tile([P, Y_BANKS], F32)
+        least_parts = keep.tile([P, 1 + len(GPSIMD_BANKS)], F32)
 
         def by_row_group(bank):
             return bank.rearrange("b (s p) -> b p s", s=ROWS_PER_PARTITION)
@@ -283,16 +296,8 @@ def tile_tnet_k_kernel(tc, x, W_fc_words, W_fc_scales, b_fc, W_q, out):
         def by_prototype(bank):
             return bank.rearrange("b (p s) -> b p s", s=ROWS_PER_PARTITION)
 
-        def clamp_and_root(T):
-            nc.vector.tensor_scalar(
-                out=clamped[:, T, :], in0=clamped[:, T, :], scalar1=floor[:, 0:1], scalar2=None,
-                op0=ALU.max, op1=ALU.min, accum_out=least_parts[:, T : T + 1],
-            )
-            nc.scalar.activation(
-                out=roots[:, T, :], in_=clamped[:, T, :], func=ACT.Abs_reciprocal_sqrt, bias=h_norm[:, 0:1]
-            )
-
-        for i, T in enumerate(GPSIMD_BANKS):
+        for i in range(Y_BANKS // 2):
+            T = GPSIMD_BANKS[i]
             multiply_half(1, T)
             nc.scalar.activation(
                 out=by_prototype(products[:, i, :]), in_=by_row_group(crosses[T][:]), func=ACT.Copy, scale=-2.0
@@ -300,17 +305,23 @@ def tile_tnet_k_kernel(tc, x, W_fc_words, W_fc_scales, b_fc, W_q, out):
             nc.gpsimd.tensor_tensor(
                 out=clamped[:, T, :], in0=products[:, i, :], in1=norms_plus_1[:, T, :], op=ALU.add
             )
-        for T in VECTOR_BANKS:
+            T = VECTOR_BANKS[i]
             multiply_half(1, T)
             nc.vector.scalar_tensor_tensor(
                 out=by_prototype(clamped[:, T, :]), in0=by_row_group(crosses[T][:]), scalar=-2.0,
                 in1=by_prototype(norms_plus_1[:, T, :]), op0=ALU.mult, op1=ALU.add,
             )
-            clamp_and_root(T)
-        for T in GPSIMD_BANKS:
-            clamp_and_root(T)
+        for i, group in enumerate([VECTOR_BANKS] + [(T,) for T in GPSIMD_BANKS]):
+            group_banks = slice(group[0], group[-1] + 1)
+            nc.vector.tensor_scalar(
+                out=clamped[:, group_banks, :], in0=clamped[:, group_banks, :], scalar1=floor[:, 0:1], scalar2=None,
+                op0=ALU.max, op1=ALU.min, accum_out=least_parts[:, i : i + 1],
+            )
+            nc.scalar.activation(
+                out=roots[:, group_banks, :], in_=clamped[:, group_banks, :], func=ACT.Abs_reciprocal_sqrt, bias=h_norm[:, 0:1]
+            )
 
-        least_terms = keep.tile([P, Y_BANKS], F32)
+        least_terms = keep.tile([P, 1 + len(GPSIMD_BANKS)], F32)
         least = keep.tile([P, 1], F32)
         nc.vector.tensor_scalar(
             out=least_terms[:], in0=least_parts[:], scalar1=h_norm[:, 0:1], scalar2=None,

from contextlib import ExitStack

import concourse.mybir as mybir
from concourse.masks import make_identity

BF16 = mybir.dt.bfloat16
F32 = mybir.dt.float32
I32 = mybir.dt.int32
U32 = mybir.dt.uint32
U8 = mybir.dt.uint8
FP8X4 = mybir.dt.float8_e4m3fn_x4
ALU = mybir.AluOpType
ACT = mybir.ActivationFunctionType
AXIS = mybir.AxisListType

P = 128
PACK = 4
K_PASS = P * PACK
WORDS = K_PASS // 2
BANK = 512

NX = 16384
NH = 1024
NY = 2048
X_PASSES = NX // K_PASS
H_PASSES = NH // K_PASS
Y_BANKS = NY // BANK

SLOT = 4096
X_CHUNKS = NX // SLOT
TILE_UNITS = 4
ROWS_PER_PARTITION = 4
SPLIT_PASSES = 6
W_LOADS = (
    [(g, 2, (0, 1)) for g in range(0, X_PASSES - SPLIT_PASSES, 2)]
    + [(g, 2, (0,)) for g in range(X_PASSES - SPLIT_PASSES, X_PASSES, 2)]
    + [(g, 2, (1,)) for g in range(X_PASSES - SPLIT_PASSES, X_PASSES - 2, 2)]
    + [(X_PASSES - 2, 1, (1,)), (X_PASSES - 1, 1, (1,))]
)
WQ_BEHIND_LOAD = (2, 4, 6, 8)
W_BUFFERS = 8
PLANES_PER_TILE = 4
NORMS_AFTER_LOAD = (X_PASSES - SPLIT_PASSES) // 2 - 2
VECTOR_BANKS = (0, 1)
GPSIMD_BANKS = (2, 3)
STORE_WIDTHS = (256, 256, 512, 512, 512)

FLOPS = 2 * P * NX * NH + 2 * P * NH * NY


def tile_tnet_k_kernel(tc, x, W_fc_words, W_fc_scales, b_fc, W_q, out):
    nc = tc.nc
    with ExitStack() as ctx:
        ctx.enter_context(tc.manual_schedule())
        keep = ctx.enter_context(tc.tile_pool(name="keep", bufs=1))
        large = ctx.enter_context(tc.tile_pool(name="large", bufs=8))
        stream = ctx.enter_context(tc.tile_pool(name="stream", bufs=W_BUFFERS))
        stage = ctx.enter_context(tc.tile_pool(name="stage", bufs=3))
        h_banks = ctx.enter_context(tc.psum_pool(name="h_banks", bufs=1))
        banks = ctx.enter_context(tc.psum_pool(name="banks", bufs=6))

        w_planes = keep.tile([P, X_PASSES // PLANES_PER_TILE, NH], U8, align_bytes=64)
        nc.vector.memset(w_planes[:].bitcast(I32), 0)
        ones = keep.tile([P, P], BF16)
        nc.vector.memset(ones[:], 1.0)
        bias_rows = keep.tile([P, NH], BF16)
        nc.vector.memset(bias_rows[:], 0.0)
        ident_f32 = keep.tile([P, P], F32)
        make_identity(nc, ident_f32[:])
        warm = keep.tile([P, 1], F32)
        nc.scalar.activation(out=warm[:], in_=ones[:, 0:1], func=ACT.Abs_reciprocal_sqrt)

        x_chunks = []
        for c in range(X_CHUNKS):
            x_chunk = large.tile([P, SLOT], BF16, tag="large", name="x_chunk%d" % c)
            nc.sync.dma_start(out=x_chunk[:], in_=x[:, SLOT * c : SLOT * (c + 1)])
            x_chunks.append(x_chunk)

        planes_words = w_planes[:].bitcast(F32)
        for a in range(X_PASSES // PLANES_PER_TILE):
            passes = slice(PLANES_PER_TILE * a, PLANES_PER_TILE * (a + 1))
            for quadrant in range(4):
                nc.gpsimd.dma_start(
                    out=planes_words[32 * quadrant : 32 * quadrant + 16, a, :],
                    in_=W_fc_scales[passes, 4 * quadrant : 4 * quadrant + 4, :].bitcast(F32),
                )

        nc.sync.dma_start(out=bias_rows[0:1, :], in_=b_fc.rearrange("(o n) -> o n", o=1))

        w_words_dram = W_fc_words.rearrange("g p n t -> p g (n t)").bitcast(I32)

        def load_w_chunk(c):
            first, passes, halves = W_LOADS[c]
            columns = slice(BANK * halves[0], BANK * (halves[-1] + 1))
            w_chunk = stream.tile([P, passes, BANK * len(halves)], U32, tag="w_chunk", name="w_chunk%d" % c, align_bytes=64)
            nc.sync.dma_start(out=w_chunk[:].bitcast(I32), in_=w_words_dram[:, first : first + passes, columns])
            w_chunks.append(w_chunk)
            if c in WQ_BEHIND_LOAD:
                T = WQ_BEHIND_LOAD.index(c)
                wq_chunk = large.tile([P, ROWS_PER_PARTITION, NH], BF16, tag="large", name="wq_chunk%d" % T)
                nc.sync.dma_start(
                    out=wq_chunk[:],
                    in_=W_q[BANK * T : BANK * (T + 1), :].rearrange("(p s) k -> p s k", s=ROWS_PER_PARTITION),
                )
                wq_chunks.append(wq_chunk)

        w_chunks = []
        wq_chunks = []
        for c in range(W_BUFFERS):
            load_w_chunk(c)

        def regroup(units):
            grouped = stage.tile([P, TILE_UNITS * K_PASS], BF16, tag="grouped", align_bytes=64)
            grouped_words = grouped[:].bitcast(F32).rearrange("p (c r u) -> p c r u", c=TILE_UNITS, u=2)
            for pair in range(TILE_UNITS // 2):
                bank = banks.tile([P, 2, 2, P], F32, tag="bank")
                for i in range(2):
                    for u in range(2):
                        nc.tensor.transpose(bank[:, i, u, :], units[2 * pair + i][:, u:WORDS:2], ident_f32[:])
                source = bank[:].rearrange("p c u r -> p c r u")
                target = grouped_words[:, 2 * pair : 2 * pair + 2]
                if pair == 0:
                    nc.vector.tensor_copy(out=target, in_=source)
                else:
                    nc.scalar.copy(out=target, in_=source)
            return grouped

        def quantise(grouped, codes, scales):
            nc.vector.quantize_mx(out=codes.bitcast(FP8X4), scales=scales, in_=grouped[:])

        a_codes = keep.tile([P, X_PASSES, P], U32, align_bytes=64)
        a_scales = keep.tile([P, X_PASSES, P], U8, align_bytes=64)
        wq_codes = keep.tile([P, H_PASSES, NY], U32, align_bytes=64)
        wq_scales = keep.tile([P, H_PASSES, NY], U8, align_bytes=64)

        waiting = None
        for c in range(X_CHUNKS):
            x_chunk = x_chunks[c]
            nc.vector.tensor_scalar_max(out=x_chunk[:], in0=x_chunk[:], scalar1=0.0)
            x_words = x_chunk[:].bitcast(F32)
            for first in range(0, SLOT // K_PASS, TILE_UNITS):
                grouped = regroup([x_words[:, WORDS * (first + i) : WORDS * (first + i + 1)] for i in range(TILE_UNITS)])
                if waiting is not None:
                    quantise(*waiting)
                g = (SLOT // K_PASS) * c + first
                waiting = (
                    grouped,
                    a_codes[:, g : g + TILE_UNITS, :].rearrange("p g b -> p (g b)"),
                    a_scales[:, g : g + TILE_UNITS, :].rearrange("p g b -> p (g b)"),
                )
        quantise(*waiting)

        bias_sorted = keep.tile([P, H_PASSES, PACK, P], F32)
        for g in range(H_PASSES):
            bias_bank = banks.tile([P, BANK], F32, tag="bank", name="bias_bank%d" % g)
            nc.tensor.matmul(
                out=bias_bank[:], lhsT=ones[:], rhs=bias_rows[:, BANK * g : BANK * (g + 1)], start=True, stop=True
            )
            nc.scalar.copy(out=bias_sorted[:, g], in_=bias_bank[:].rearrange("b (p t) -> b t p", t=PACK))

        wq_norms = keep.tile([P, Y_BANKS * ROWS_PER_PARTITION], F32)

        def work_up_wq(T):
            wq_words = wq_chunks[T][:].bitcast(F32)
            grouped = [
                regroup([wq_words[:, s, WORDS * g : WORDS * (g + 1)] for s in range(ROWS_PER_PARTITION)])
                for g in range(H_PASSES)
            ]
            for g in range(H_PASSES):
                quantise(grouped[g], wq_codes[:, g, BANK * T : BANK * (T + 1)], wq_scales[:, g, BANK * T : BANK * (T + 1)])
            for s in range(ROWS_PER_PARTITION):
                squares = stage.tile([P, NH], BF16, tag="squares")
                column = ROWS_PER_PARTITION * T + s
                row = wq_chunks[T][:, s, :]
                if s % 2 == 0:
                    nc.scalar.activation(
                        out=squares[:], in_=row, func=ACT.Square, accum_out=wq_norms[:, column : column + 1]
                    )
                else:
                    nc.vector.scalar_tensor_tensor(
                        out=squares[:], in0=row, scalar=1.0, in1=row, op0=ALU.mult, op1=ALU.mult,
                        accum_out=wq_norms[:, column : column + 1],
                    )

        pre = keep.tile([P, H_PASSES, PACK, P], F32)
        h_squares = keep.tile([P, H_PASSES, K_PASS], F32)
        h_norm_parts = keep.tile([P, H_PASSES], F32)
        floor_part = keep.tile([P, 1], F32)
        h_grouped = keep.tile([P, H_PASSES, P, PACK], BF16, align_bytes=64)
        h_codes = keep.tile([P, H_PASSES, P], U32, align_bytes=64)
        h_scales = keep.tile([P, H_PASSES, P], U8, align_bytes=64)

        def add_bias(g):
            nc.vector.tensor_tensor(
                out=pre[:, g], in0=h_acc[g][:].rearrange("b (p t) -> b t p", t=PACK), in1=bias_sorted[:, g], op=ALU.add
            )
            flat = pre[:, g].rearrange("b t p -> b (t p)")
            nc.vector.scalar_tensor_tensor(
                out=h_squares[:, g, :], in0=flat, scalar=0.0, in1=flat, op0=ALU.max, op1=ALU.mult,
                accum_out=h_norm_parts[:, g : g + 1],
            )
            if g == 0:
                nc.vector.tensor_scalar(
                    out=floor_part[:], in0=h_norm_parts[:, 0:1], scalar1=-1.0, scalar2=1.0, op0=ALU.mult, op1=ALU.add
                )

        def transpose_half(g):
            for first in range(0, PACK, 2):
                pre_T = banks.tile([P, 2, P], F32, tag="bank")
                for i in range(2):
                    nc.tensor.transpose(pre_T[:, i, :], pre[:, g, first + i, :], ident_f32[:])
                target = h_grouped[:, g, :, first : first + 2]
                source = pre_T[:].rearrange("p t b -> p b t")
                if first == 0:
                    nc.scalar.activation(out=target, in_=source, func=ACT.Relu)
                else:
                    nc.vector.tensor_scalar_max(out=target, in0=source, scalar1=0.0)
            nc.vector.quantize_mx(
                out=h_codes[:, g, :].bitcast(FP8X4),
                scales=h_scales[:, g, :],
                in_=h_grouped[:, g].rearrange("p b t -> p (b t)"),
            )

        h_acc = [h_banks.tile([P, BANK], F32, name="h_acc%d" % n) for n in range(H_PASSES)]
        norms_plus_1 = None
        for c, (first, passes, halves) in enumerate(W_LOADS):
            for i in range(passes):
                g = first + i
                plane_start = 4 * (g % PLANES_PER_TILE)
                for n in halves:
                    start = BANK * (n - halves[0])
                    nc.tensor.matmul_mx(
                        out=h_acc[n][:],
                        lhsT=a_codes[:, g, :].bitcast(FP8X4),
                        lhsT_scale=a_scales[:, g, :],
                        rhs=w_chunks[c][:, i, start : start + BANK].bitcast(FP8X4),
                        rhs_scale=w_planes[plane_start:P, g // PLANES_PER_TILE, BANK * n : BANK * (n + 1)],
                        start=(g == 0),
                        stop=(g == X_PASSES - 1),
                    )
                if g == X_PASSES - 1:
                    add_bias(halves[-1])
            if c + W_BUFFERS < len(W_LOADS):
                load_w_chunk(c + W_BUFFERS)
            if c in WQ_BEHIND_LOAD:
                work_up_wq(WQ_BEHIND_LOAD.index(c))
            if first == X_PASSES - SPLIT_PASSES and halves == (1,):
                transpose_half(0)

            if c == NORMS_AFTER_LOAD:
                norms_plus_1 = large.tile([P, Y_BANKS, BANK], F32, tag="large")
                for T in range(Y_BANKS):
                    norm_bank = banks.tile([P, ROWS_PER_PARTITION, P], F32, tag="bank")
                    for s in range(ROWS_PER_PARTITION):
                        column = ROWS_PER_PARTITION * T + s
                        nc.tensor.transpose(
                            norm_bank[:, s, :], wq_norms[:, column : column + 1].to_broadcast([P, P]), ident_f32[:]
                        )
                    nc.vector.tensor_scalar_add(
                        out=norms_plus_1[:, T, :].rearrange("b (p s) -> b p s", s=ROWS_PER_PARTITION),
                        in0=norm_bank[:].rearrange("b s p -> b p s"),
                        scalar1=1.0,
                    )

        crosses = [banks.tile([P, BANK], F32, tag="bank", name="cross%d" % T) for T in range(Y_BANKS)]

        def multiply_half(g, T):
            nc.tensor.matmul_mx(
                out=crosses[T][:],
                lhsT=h_codes[:, g, :].bitcast(FP8X4),
                lhsT_scale=h_scales[:, g, :],
                rhs=wq_codes[:, g, BANK * T : BANK * (T + 1)].bitcast(FP8X4),
                rhs_scale=wq_scales[:, g, BANK * T : BANK * (T + 1)],
                start=(g == 0),
                stop=(g == H_PASSES - 1),
            )

        bank_order = [T for pair in zip(GPSIMD_BANKS, VECTOR_BANKS) for T in pair]
        for T in bank_order[:-1]:
            multiply_half(0, T)
        transpose_half(1)
        h_norm = keep.tile([P, 1], F32)
        nc.vector.tensor_add(out=h_norm[:], in0=h_norm_parts[:, 0:1], in1=h_norm_parts[:, 1:2])
        floor = keep.tile([P, 1], F32)
        nc.vector.tensor_sub(out=floor[:], in0=floor_part[:], in1=h_norm_parts[:, 1:2])
        multiply_half(0, bank_order[-1])

        clamped = large.tile([P, Y_BANKS, BANK], F32, tag="large")
        products = large.tile([P, len(GPSIMD_BANKS), BANK], F32, tag="large")
        roots = large.tile([P, Y_BANKS, BANK], F32, tag="large")
        least_parts = keep.tile([P, 1 + len(GPSIMD_BANKS)], F32)

        def by_row_group(bank):
            return bank.rearrange("b (s p) -> b p s", s=ROWS_PER_PARTITION)

        def by_prototype(bank):
            return bank.rearrange("b (p s) -> b p s", s=ROWS_PER_PARTITION)

        for i in range(Y_BANKS // 2):
            T = GPSIMD_BANKS[i]
            multiply_half(1, T)
            nc.scalar.activation(
                out=by_prototype(products[:, i, :]), in_=by_row_group(crosses[T][:]), func=ACT.Copy, scale=-2.0
            )
            nc.gpsimd.tensor_tensor(
                out=clamped[:, T, :], in0=products[:, i, :], in1=norms_plus_1[:, T, :], op=ALU.add
            )
            T = VECTOR_BANKS[i]
            multiply_half(1, T)
            nc.vector.scalar_tensor_tensor(
                out=by_prototype(clamped[:, T, :]), in0=by_row_group(crosses[T][:]), scalar=-2.0,
                in1=by_prototype(norms_plus_1[:, T, :]), op0=ALU.mult, op1=ALU.add,
            )
        for i, group in enumerate([VECTOR_BANKS] + [(T,) for T in GPSIMD_BANKS]):
            group_banks = slice(group[0], group[-1] + 1)
            nc.vector.tensor_scalar(
                out=clamped[:, group_banks, :], in0=clamped[:, group_banks, :], scalar1=floor[:, 0:1], scalar2=None,
                op0=ALU.max, op1=ALU.min, accum_out=least_parts[:, i : i + 1],
            )
            nc.scalar.activation(
                out=roots[:, group_banks, :], in_=clamped[:, group_banks, :], func=ACT.Abs_reciprocal_sqrt, bias=h_norm[:, 0:1]
            )

        least_terms = keep.tile([P, 1 + len(GPSIMD_BANKS)], F32)
        least = keep.tile([P, 1], F32)
        nc.vector.tensor_scalar(
            out=least_terms[:], in0=least_parts[:], scalar1=h_norm[:, 0:1], scalar2=None,
            op0=ALU.add, op1=ALU.min, accum_out=least[:],
        )
        terms = large.tile([P, NY], F32, tag="large")
        total_parts = keep.tile([P, 2], F32)
        roots_flat = roots[:].rearrange("b T j -> b (T j)")
        for part, columns in enumerate([slice(0, NY - BANK), slice(NY - BANK, NY)]):
            nc.vector.scalar_tensor_tensor(
                out=terms[:, columns], in0=roots_flat[:, columns], scalar=least[:, 0:1], in1=roots_flat[:, columns],
                op0=ALU.mult, op1=ALU.mult, accum_out=total_parts[:, part : part + 1],
            )

        logs = large.tile([P, NY], F32, tag="large")
        log_total = keep.tile([P, 1], F32)
        for T in range(Y_BANKS):
            columns = slice(BANK * T, BANK * (T + 1))
            nc.scalar.activation(out=logs[:, columns], in_=terms[:, columns], func=ACT.Ln)
            if T == 0:
                nc.scalar.activation(
                    out=log_total[:], in_=total_parts[:, 0:1], func=ACT.Ln, bias=total_parts[:, 1:2]
                )
        result = large.tile([P, NY], F32, tag="large")
        first = 0
        for width in STORE_WIDTHS:
            columns = slice(first, first + width)
            nc.vector.tensor_scalar_sub(out=result[:, columns], in0=logs[:, columns], scalar1=log_total[:, 0:1])
            nc.sync.dma_start(out=out[:, columns], in_=result[:, columns])
            first += width
